import numpy as np
import ml_dtypes


def mxq(x, axis, fmt="e4m3"):
    dtype, down = {"e4m3": (ml_dtypes.float8_e4m3fn, 7), "e5m2": (ml_dtypes.float8_e5m2, 14)}[fmt]
    v = np.moveaxis(np.asarray(x, np.float32).astype(ml_dtypes.bfloat16).astype(np.float64), axis, -1)
    blocks = v.reshape(v.shape[:-1] + (-1, 32))
    amax = np.abs(blocks).max(-1, keepdims=True)
    byte = np.maximum(np.where(amax > 0, np.frexp(amax)[1] - 1 + 127, 0) - down, 1)
    scale = np.exp2(byte - 127.0)
    codes = (blocks / scale).astype(np.float32).astype(dtype).astype(np.float64)
    return np.moveaxis((codes * scale).reshape(v.shape), -1, axis)


WIDE = False


def mx_kscale(k):
    if not WIDE:
        return np.ones(k)
    levels = np.array([10, -10, 5, -5, 0])
    a = np.random.permutation(np.resize(levels, k // 512 * 4)).reshape(k // 512, 4)
    idx = np.arange(k)
    return np.exp2(a[idx // 512, idx % 128 // 32])


BF16 = ml_dtypes.bfloat16


def bf(x):
    return np.asarray(x, np.float32).astype(BF16)


def f64(x):
    return np.asarray(x).astype(np.float64)


B, P0, P1, P2, K0, K1, K2 = 4096, 128, 128, 128, 512, 512, 512
PT = P0 + P1 + P2
KT = K0 + K1 + K2
CLIP1 = 1.0


def clip_rows(mat, clip):
    norms = np.sqrt(np.sum(mat * mat, axis=1, keepdims=True))
    scale = np.minimum(clip / norms, 1.0)
    return mat * scale


def setup_inputs():
    t0, t1, t2 = mx_kscale(K0), mx_kscale(K1), mx_kscale(K2)
    r = np.exp2(np.random.uniform(-2.0, 2.0, (B, 1))) / (KT * PT) ** 0.25
    return {"target_grad": bf(np.random.standard_normal((B, PT)) * r),
            "embedding": bf(np.random.standard_normal((B, KT)) * r * np.concatenate([t0, t1, t2])),
            "bases0": bf(np.random.standard_normal((P0, K0)) / np.sqrt(P0) / t0[None, :]),
            "bases1": bf(np.random.standard_normal((P1, K1)) / np.sqrt(P1) / t1[None, :]),
            "bases2": bf(np.random.standard_normal((P2, K2)) / np.sqrt(P2) / t2[None, :])}


def reference(target_grad, embedding, bases0, bases1, bases2):
    g = f64(target_grad)
    e = f64(embedding)
    approx_parts = []
    offset = 0
    for b in (f64(bases0), f64(bases1), f64(bases2)):
        num_k = b.shape[1]
        approx_parts.append(mxq(e[:, offset:offset + num_k], 1, "e4m3") @ mxq(b.T, 0, "e4m3"))
        offset += num_k
    no_reduction_approx = np.concatenate(approx_parts, axis=1)
    residual = g - no_reduction_approx
    return np.sum(clip_rows(residual, CLIP1), axis=0) / B

@@ -1,0 +1,203 @@
+from contextlib import ExitStack
+
+import concourse.mybir as mybir
+from concourse.masks import make_identity
+
+F32 = mybir.dt.float32
+BF16 = mybir.dt.bfloat16
+U32 = mybir.dt.uint32
+U8 = mybir.dt.uint8
+FP8X4 = mybir.dt.float8_e4m3fn_x4
+ALU = mybir.AluOpType
+ACT = mybir.ActivationFunctionType
+AXIS = mybir.AxisListType
+
+P = 128
+BATCH = 4096
+GROUPS = 3
+K_GROUP = 512
+K_ALL = GROUPS * K_GROUP
+J_ALL = GROUPS * P
+TILES = BATCH // P
+STEP_TILES = 2
+STEPS = TILES // STEP_TILES
+STEP_UNITS = STEP_TILES * GROUPS
+UNIT_WORDS = K_GROUP // 2
+BANK_UNITS = 2
+STEP_BANKS = STEP_UNITS // BANK_UNITS
+QUANTISE_LAG = 1
+MULTIPLY_LAG = 2
+SQUARE_LAG = 3
+WEIGH_LAG = 5
+VECTOR_COPY_EVERY = 6
+
+FLOPS = 2 * BATCH * K_ALL * P
+
+
+def tile_gep_pb_t_kernel(tc, target_grad, embedding, bases0, bases1, bases2, out):
+    nc = tc.nc
+    with ExitStack() as ctx:
+        ctx.enter_context(tc.manual_schedule())
+        const = ctx.enter_context(tc.tile_pool(name="const", bufs=1))
+        e_pool = ctx.enter_context(tc.tile_pool(name="e_pool", bufs=STEPS))
+        g_pool = ctx.enter_context(tc.tile_pool(name="g_pool", bufs=STEPS))
+        grouped_pool = ctx.enter_context(tc.tile_pool(name="grouped_pool", bufs=3))
+        mx_pool = ctx.enter_context(tc.tile_pool(name="mx_pool", bufs=3))
+        resid_pool = ctx.enter_context(tc.tile_pool(name="resid_pool", bufs=WEIGH_LAG - MULTIPLY_LAG + 3))
+        small_pool = ctx.enter_context(tc.tile_pool(name="small_pool", bufs=5))
+        flip_psum = ctx.enter_context(tc.psum_pool(name="flip_psum", bufs=4))
+        approx_psum = ctx.enter_context(tc.psum_pool(name="approx_psum", bufs=3))
+        sums_psum = ctx.enter_context(tc.psum_pool(name="sums_psum", bufs=1))
+
+        emb_rows = embedding.rearrange("(p t) k -> p (t k)", t=TILES)
+        grad_rows = target_grad.rearrange("(p t) j -> p (t j)", t=TILES)
+        b_raw = const.tile([P, K_ALL], BF16)
+        for g, bases in enumerate((bases0, bases1, bases2)):
+            nc.scalar.dma_start(out=b_raw[:, g * K_GROUP : (g + 1) * K_GROUP], in_=bases)
+        e_raw = []
+        g_raw = []
+        for s in range(STEPS):
+            e_step = e_pool.tile([P, STEP_TILES * K_ALL], BF16)
+            nc.sync.dma_start(out=e_step[:], in_=emb_rows[:, s * STEP_TILES * K_ALL : (s + 1) * STEP_TILES * K_ALL])
+            e_raw.append(e_step)
+            g_step = g_pool.tile([P, STEP_TILES * J_ALL], BF16)
+            nc.sync.dma_start(out=g_step[:], in_=grad_rows[:, s * STEP_TILES * J_ALL : (s + 1) * STEP_TILES * J_ALL])
+            g_raw.append(g_step)
+
+        ident = const.tile([P, P], F32)
+        make_identity(nc, ident[:])
+        totals = const.tile([P, P], F32)
+        nc.vector.memset(totals[:], 0.0)
+        minus_half = const.tile([P, STEP_TILES], F32)
+        nc.gpsimd.memset(minus_half[:], -0.5)
+
+        def flip_units(src, grouped, first_unit, n_units, on_vector):
+            src_words = src[:].bitcast(F32)
+            grouped_words = grouped[:].bitcast(F32)
+            flipped = flip_psum.tile([P, BANK_UNITS, 2, P], F32)
+            for n in range(n_units):
+                for h in range(2):
+                    first_word = (first_unit + n) * UNIT_WORDS + h * P
+                    nc.tensor.transpose(flipped[:, n, h, :], src_words[:, first_word : first_word + P], ident[:])
+            dst = grouped_words[:, first_unit * UNIT_WORDS : (first_unit + n_units) * UNIT_WORDS]
+            dst = dst.rearrange("p (n r h) -> p n r h", n=n_units, h=2)
+            flipped_rows = flipped[:, 0:n_units, :, :].rearrange("p n h r -> p n r h")
+            if on_vector:
+                nc.vector.tensor_copy(out=dst, in_=flipped_rows)
+            else:
+                nc.scalar.copy(out=dst, in_=flipped_rows)
+
+        def quantise_units(grouped, codes, scales, first_unit, n_units):
+            cols = slice(first_unit * P, (first_unit + n_units) * P)
+            nc.vector.quantize_mx(
+                out=codes[:, cols].bitcast(FP8X4),
+                scales=scales[:, cols],
+                in_=grouped[:, first_unit * K_GROUP : (first_unit + n_units) * K_GROUP],
+            )
+
+        b_grouped = const.tile([P, K_ALL], BF16, align_bytes=64)
+        b_codes = const.tile([P, J_ALL], U32, align_bytes=64)
+        b_scales = const.tile([P, J_ALL], U8, align_bytes=64)
+        for g in range(GROUPS):
+            flip_units(b_raw, b_grouped, g, 1, False)
+        for g in range(GROUPS):
+            quantise_units(b_grouped, b_codes, b_scales, g, 1)
+
+        grouped_of = {}
+        codes_of = {}
+        scales_of = {}
+        resid_of = {}
+        sumsq_of = {}
+        factor_of = {}
+        sums = sums_psum.tile([P, GROUPS * STEPS], F32)
+
+        def flip(s):
+            grouped = grouped_pool.tile([P, STEP_UNITS * K_GROUP], BF16, align_bytes=64)
+            grouped_of[s] = grouped
+            for bank in range(STEP_BANKS):
+                on_vector = (s * STEP_BANKS + bank) % VECTOR_COPY_EVERY == VECTOR_COPY_EVERY - 1
+                flip_units(e_raw[s], grouped, bank * BANK_UNITS, BANK_UNITS, on_vector)
+
+        def quantise(s):
+            codes = mx_pool.tile([P, STEP_UNITS * P], U32, align_bytes=64)
+            scales = mx_pool.tile([P, STEP_UNITS * P], U8, align_bytes=64)
+            codes_of[s] = codes
+            scales_of[s] = scales
+            for bank in range(STEP_BANKS):
+                quantise_units(grouped_of[s], codes, scales, bank * BANK_UNITS, BANK_UNITS)
+
+        def multiply(s):
+            resid = resid_pool.tile([P, STEP_TILES * J_ALL], F32)
+            resid_of[s] = resid
+            for t in range(STEP_TILES):
+                approx = approx_psum.tile([P, J_ALL], F32)
+                for g in range(GROUPS):
+                    unit_cols = slice((t * GROUPS + g) * P, (t * GROUPS + g + 1) * P)
+                    g_cols = slice(g * P, (g + 1) * P)
+                    nc.tensor.matmul_mx(
+                        out=approx[:, g_cols],
+                        lhsT=codes_of[s][:, unit_cols].bitcast(FP8X4),
+                        lhsT_scale=scales_of[s][:, unit_cols],
+                        rhs=b_codes[:, g_cols].bitcast(FP8X4),
+                        rhs_scale=b_scales[:, g_cols],
+                        start=True,
+                        stop=True,
+                    )
+                t_cols = slice(t * J_ALL, (t + 1) * J_ALL)
+                nc.vector.tensor_tensor(out=resid[:, t_cols], in0=g_raw[s][:, t_cols], in1=approx[:], op=ALU.subtract)
+
+        def square(s):
+            sumsq = small_pool.tile([P, STEP_TILES], F32)
+            sumsq_of[s] = sumsq
+            for t in range(STEP_TILES):
+                squares = small_pool.tile([P, J_ALL], BF16)
+                nc.scalar.activation(
+                    out=squares[:],
+                    in_=resid_of[s][:, t * J_ALL : (t + 1) * J_ALL],
+                    func=ACT.Square,
+                    accum_out=sumsq[:, t : t + 1],
+                )
+
+        def clip_factor(s):
+            floored = small_pool.tile([P, STEP_TILES], F32)
+            nc.gpsimd.tensor_scalar_max(out=floored[:], in0=sumsq_of[s][:], scalar1=1.0)
+            factor = small_pool.tile([P, STEP_TILES], F32)
+            nc.gpsimd.tensor_tensor(out=factor[:], in0=floored[:], in1=minus_half[:], op=ALU.pow)
+            factor_of[s] = factor
+
+        def weigh(s):
+            for g in range(GROUPS):
+                for t in range(STEP_TILES):
+                    unit_cols = slice((t * GROUPS + g) * P, (t * GROUPS + g + 1) * P)
+                    nc.tensor.matmul(
+                        out=sums[:, g * STEPS + s : g * STEPS + s + 1],
+                        lhsT=resid_of[s][:, unit_cols],
+                        rhs=factor_of[s][:, t : t + 1],
+                        start=(t == 0),
+                        stop=(t == STEP_TILES - 1),
+                    )
+
+        for turn in range(STEPS + WEIGH_LAG):
+            if 0 <= turn - QUANTISE_LAG < STEPS:
+                quantise(turn - QUANTISE_LAG)
+            if turn < STEPS:
+                flip(turn)
+            if 0 <= turn - MULTIPLY_LAG < STEPS:
+                multiply(turn - MULTIPLY_LAG)
+            if 0 <= turn - SQUARE_LAG < STEPS:
+                square(turn - SQUARE_LAG)
+                clip_factor(turn - SQUARE_LAG)
+            if 0 <= turn - WEIGH_LAG < STEPS:
+                weigh(turn - WEIGH_LAG)
+
+        nc.vector.tensor_reduce(
+            out=totals[:, 0:GROUPS],
+            in_=sums[:].rearrange("p (g s) -> p g s", g=GROUPS),
+            axis=AXIS.X,
+            op=ALU.add,
+        )
+        totals_flipped = flip_psum.tile([P, P], F32, tag="flipped")
+        nc.tensor.transpose(totals_flipped[:], totals[:], ident[:])
+        mean = const.tile([P, P], F32)
+        nc.scalar.mul(out=mean[:], in_=totals_flipped[:], mul=1.0 / BATCH)
+        nc.sync.dma_start(out=out.rearrange("(g j) -> g j", g=GROUPS), in_=mean[0:GROUPS, :])

@@ -10,7 +10,6 @@ U8 = mybir.dt.uint8
 FP8X4 = mybir.dt.float8_e4m3fn_x4
 ALU = mybir.AluOpType
 ACT = mybir.ActivationFunctionType
-AXIS = mybir.AxisListType
 
 P = 128
 BATCH = 4096
@@ -29,7 +28,6 @@ QUANTISE_LAG = 1
 MULTIPLY_LAG = 2
 SQUARE_LAG = 3
 WEIGH_LAG = 5
-VECTOR_COPY_EVERY = 6
 
 FLOPS = 2 * BATCH * K_ALL * P
 
@@ -47,7 +45,6 @@ def tile_gep_pb_t_kernel(tc, target_grad, embedding, bases0, bases1, bases2, out
         small_pool = ctx.enter_context(tc.tile_pool(name="small_pool", bufs=5))
         flip_psum = ctx.enter_context(tc.psum_pool(name="flip_psum", bufs=4))
         approx_psum = ctx.enter_context(tc.psum_pool(name="approx_psum", bufs=3))
-        sums_psum = ctx.enter_context(tc.psum_pool(name="sums_psum", bufs=1))
 
         emb_rows = embedding.rearrange("(p t) k -> p (t k)", t=TILES)
         grad_rows = target_grad.rearrange("(p t) j -> p (t j)", t=TILES)
@@ -66,12 +63,17 @@ def tile_gep_pb_t_kernel(tc, target_grad, embedding, bases0, bases1, bases2, out
 
         ident = const.tile([P, P], F32)
         make_identity(nc, ident[:])
-        totals = const.tile([P, P], F32)
-        nc.vector.memset(totals[:], 0.0)
+        ones = const.tile([P, P], F32)
+        nc.vector.memset(ones[:], 1.0)
+        weighted = []
+        for t in range(STEP_TILES):
+            weighted_t = const.tile([P, J_ALL], F32, name="weighted_%d" % t)
+            nc.vector.memset(weighted_t[:], 0.0)
+            weighted.append(weighted_t)
         minus_half = const.tile([P, STEP_TILES], F32)
         nc.gpsimd.memset(minus_half[:], -0.5)
 
-        def flip_units(src, grouped, first_unit, n_units, on_vector):
+        def flip_units(src, grouped, first_unit, n_units):
             src_words = src[:].bitcast(F32)
             grouped_words = grouped[:].bitcast(F32)
             flipped = flip_psum.tile([P, BANK_UNITS, 2, P], F32)
@@ -82,10 +84,7 @@ def tile_gep_pb_t_kernel(tc, target_grad, embedding, bases0, bases1, bases2, out
             dst = grouped_words[:, first_unit * UNIT_WORDS : (first_unit + n_units) * UNIT_WORDS]
             dst = dst.rearrange("p (n r h) -> p n r h", n=n_units, h=2)
             flipped_rows = flipped[:, 0:n_units, :, :].rearrange("p n h r -> p n r h")
-            if on_vector:
-                nc.vector.tensor_copy(out=dst, in_=flipped_rows)
-            else:
-                nc.scalar.copy(out=dst, in_=flipped_rows)
+            nc.scalar.copy(out=dst, in_=flipped_rows)
 
         def quantise_units(grouped, codes, scales, first_unit, n_units):
             cols = slice(first_unit * P, (first_unit + n_units) * P)
@@ -99,7 +98,7 @@ def tile_gep_pb_t_kernel(tc, target_grad, embedding, bases0, bases1, bases2, out
         b_codes = const.tile([P, J_ALL], U32, align_bytes=64)
         b_scales = const.tile([P, J_ALL], U8, align_bytes=64)
         for g in range(GROUPS):
-            flip_units(b_raw, b_grouped, g, 1, False)
+            flip_units(b_raw, b_grouped, g, 1)
         for g in range(GROUPS):
             quantise_units(b_grouped, b_codes, b_scales, g, 1)
 
@@ -109,14 +108,12 @@ def tile_gep_pb_t_kernel(tc, target_grad, embedding, bases0, bases1, bases2, out
         resid_of = {}
         sumsq_of = {}
         factor_of = {}
-        sums = sums_psum.tile([P, GROUPS * STEPS], F32)
 
         def flip(s):
             grouped = grouped_pool.tile([P, STEP_UNITS * K_GROUP], BF16, align_bytes=64)
             grouped_of[s] = grouped
             for bank in range(STEP_BANKS):
-                on_vector = (s * STEP_BANKS + bank) % VECTOR_COPY_EVERY == VECTOR_COPY_EVERY - 1
-                flip_units(e_raw[s], grouped, bank * BANK_UNITS, BANK_UNITS, on_vector)
+                flip_units(e_raw[s], grouped, bank * BANK_UNITS, BANK_UNITS)
 
         def quantise(s):
             codes = mx_pool.tile([P, STEP_UNITS * P], U32, align_bytes=64)
@@ -166,16 +163,15 @@ def tile_gep_pb_t_kernel(tc, target_grad, embedding, bases0, bases1, bases2, out
             factor_of[s] = factor
 
         def weigh(s):
-            for g in range(GROUPS):
-                for t in range(STEP_TILES):
-                    unit_cols = slice((t * GROUPS + g) * P, (t * GROUPS + g + 1) * P)
-                    nc.tensor.matmul(
-                        out=sums[:, g * STEPS + s : g * STEPS + s + 1],
-                        lhsT=resid_of[s][:, unit_cols],
-                        rhs=factor_of[s][:, t : t + 1],
-                        start=(t == 0),
-                        stop=(t == STEP_TILES - 1),
-                    )
+            for t in range(STEP_TILES):
+                nc.vector.scalar_tensor_tensor(
+                    out=weighted[t][:],
+                    in0=resid_of[s][:, t * J_ALL : (t + 1) * J_ALL],
+                    scalar=factor_of[s][:, t : t + 1],
+                    in1=weighted[t][:],
+                    op0=ALU.mult,
+                    op1=ALU.add,
+                )
 
         for turn in range(STEPS + WEIGH_LAG):
             if 0 <= turn - QUANTISE_LAG < STEPS:
@@ -190,14 +186,10 @@ def tile_gep_pb_t_kernel(tc, target_grad, embedding, bases0, bases1, bases2, out
             if 0 <= turn - WEIGH_LAG < STEPS:
                 weigh(turn - WEIGH_LAG)
 
-        nc.vector.tensor_reduce(
-            out=totals[:, 0:GROUPS],
-            in_=sums[:].rearrange("p (g s) -> p g s", g=GROUPS),
-            axis=AXIS.X,
-            op=ALU.add,
-        )
-        totals_flipped = flip_psum.tile([P, P], F32, tag="flipped")
-        nc.tensor.transpose(totals_flipped[:], totals[:], ident[:])
-        mean = const.tile([P, P], F32)
-        nc.scalar.mul(out=mean[:], in_=totals_flipped[:], mul=1.0 / BATCH)
-        nc.sync.dma_start(out=out.rearrange("(g j) -> g j", g=GROUPS), in_=mean[0:GROUPS, :])
+        for t in range(1, STEP_TILES):
+            nc.vector.tensor_tensor(out=weighted[0][:], in0=weighted[0][:], in1=weighted[t][:], op=ALU.add)
+        column_sums = approx_psum.tile([P, J_ALL], F32, tag="approx")
+        nc.tensor.matmul(out=column_sums[:], lhsT=ones[:], rhs=weighted[0][:], start=True, stop=True)
+        mean = const.tile([P, J_ALL], F32)
+        nc.scalar.mul(out=mean[:], in_=column_sums[:], mul=1.0 / BATCH)
+        nc.sync.dma_start(out=out.rearrange("(o j) -> o j", o=1), in_=mean[0:1, :])

@@ -18,16 +18,21 @@ K_GROUP = 512
 K_ALL = GROUPS * K_GROUP
 J_ALL = GROUPS * P
 TILES = BATCH // P
-STEP_TILES = 2
+STEP_TILES = 4
 STEPS = TILES // STEP_TILES
 STEP_UNITS = STEP_TILES * GROUPS
+STEP_COLS = STEP_TILES * J_ALL
 UNIT_WORDS = K_GROUP // 2
-BANK_UNITS = 2
-STEP_BANKS = STEP_UNITS // BANK_UNITS
+FLIP_UNITS = 2
+LOAD_TILES = 2
+LOAD_UNITS = LOAD_TILES * GROUPS
+STEP_LOADS = STEP_TILES // LOAD_TILES
+BANK_COLS = 512
+PRODUCT_UNITS = BANK_COLS // P
 QUANTISE_LAG = 1
 MULTIPLY_LAG = 2
-SQUARE_LAG = 3
-WEIGH_LAG = 5
+SQUARE_LAG = 2
+WEIGH_LAG = 4
 
 FLOPS = 2 * BATCH * K_ALL * P
 
@@ -37,13 +42,13 @@ def tile_gep_pb_t_kernel(tc, target_grad, embedding, bases0, bases1, bases2, out
     with ExitStack() as ctx:
         ctx.enter_context(tc.manual_schedule())
         const = ctx.enter_context(tc.tile_pool(name="const", bufs=1))
-        e_pool = ctx.enter_context(tc.tile_pool(name="e_pool", bufs=STEPS))
+        e_pool = ctx.enter_context(tc.tile_pool(name="e_pool", bufs=STEPS * STEP_LOADS))
         g_pool = ctx.enter_context(tc.tile_pool(name="g_pool", bufs=STEPS))
-        grouped_pool = ctx.enter_context(tc.tile_pool(name="grouped_pool", bufs=3))
+        grouped_pool = ctx.enter_context(tc.tile_pool(name="grouped_pool", bufs=2))
         mx_pool = ctx.enter_context(tc.tile_pool(name="mx_pool", bufs=3))
-        resid_pool = ctx.enter_context(tc.tile_pool(name="resid_pool", bufs=WEIGH_LAG - MULTIPLY_LAG + 3))
+        resid_pool = ctx.enter_context(tc.tile_pool(name="resid_pool", bufs=WEIGH_LAG - MULTIPLY_LAG + 2))
         small_pool = ctx.enter_context(tc.tile_pool(name="small_pool", bufs=5))
-        flip_psum = ctx.enter_context(tc.psum_pool(name="flip_psum", bufs=4))
+        flip_psum = ctx.enter_context(tc.psum_pool(name="flip_psum", bufs=5))
         approx_psum = ctx.enter_context(tc.psum_pool(name="approx_psum", bufs=3))
 
         emb_rows = embedding.rearrange("(p t) k -> p (t k)", t=TILES)
@@ -54,11 +59,12 @@ def tile_gep_pb_t_kernel(tc, target_grad, embedding, bases0, bases1, bases2, out
         e_raw = []
         g_raw = []
         for s in range(STEPS):
-            e_step = e_pool.tile([P, STEP_TILES * K_ALL], BF16)
-            nc.sync.dma_start(out=e_step[:], in_=emb_rows[:, s * STEP_TILES * K_ALL : (s + 1) * STEP_TILES * K_ALL])
-            e_raw.append(e_step)
-            g_step = g_pool.tile([P, STEP_TILES * J_ALL], BF16)
-            nc.sync.dma_start(out=g_step[:], in_=grad_rows[:, s * STEP_TILES * J_ALL : (s + 1) * STEP_TILES * J_ALL])
+            for load in range(s * STEP_LOADS, (s + 1) * STEP_LOADS):
+                e_load = e_pool.tile([P, LOAD_TILES * K_ALL], BF16)
+                nc.sync.dma_start(out=e_load[:], in_=emb_rows[:, load * LOAD_TILES * K_ALL : (load + 1) * LOAD_TILES * K_ALL])
+                e_raw.append(e_load)
+            g_step = g_pool.tile([P, STEP_COLS], BF16)
+            nc.sync.dma_start(out=g_step[:], in_=grad_rows[:, s * STEP_COLS : (s + 1) * STEP_COLS])
             g_raw.append(g_step)
 
         ident = const.tile([P, P], F32)
@@ -66,20 +72,20 @@ def tile_gep_pb_t_kernel(tc, target_grad, embedding, bases0, bases1, bases2, out
         ones = const.tile([P, P], F32)
         nc.vector.memset(ones[:], 1.0)
         weighted = []
-        for t in range(STEP_TILES):
+        for t in range(2):
             weighted_t = const.tile([P, J_ALL], F32, name="weighted_%d" % t)
             nc.vector.memset(weighted_t[:], 0.0)
             weighted.append(weighted_t)
         minus_half = const.tile([P, STEP_TILES], F32)
         nc.gpsimd.memset(minus_half[:], -0.5)
 
-        def flip_units(src, grouped, first_unit, n_units):
+        def flip_units(src, src_unit, grouped, first_unit, n_units):
             src_words = src[:].bitcast(F32)
             grouped_words = grouped[:].bitcast(F32)
-            flipped = flip_psum.tile([P, BANK_UNITS, 2, P], F32)
+            flipped = flip_psum.tile([P, FLIP_UNITS, 2, P], F32)
             for n in range(n_units):
                 for h in range(2):
-                    first_word = (first_unit + n) * UNIT_WORDS + h * P
+                    first_word = (src_unit + n) * UNIT_WORDS + h * P
                     nc.tensor.transpose(flipped[:, n, h, :], src_words[:, first_word : first_word + P], ident[:])
             dst = grouped_words[:, first_unit * UNIT_WORDS : (first_unit + n_units) * UNIT_WORDS]
             dst = dst.rearrange("p (n r h) -> p n r h", n=n_units, h=2)
@@ -98,7 +104,7 @@ def tile_gep_pb_t_kernel(tc, target_grad, embedding, bases0, bases1, bases2, out
         b_codes = const.tile([P, J_ALL], U32, align_bytes=64)
         b_scales = const.tile([P, J_ALL], U8, align_bytes=64)
         for g in range(GROUPS):
-            flip_units(b_raw, b_grouped, g, 1)
+            flip_units(b_raw, g, b_grouped, g, 1)
         for g in range(GROUPS):
             quantise_units(b_grouped, b_codes, b_scales, g, 1)
 
@@ -112,36 +118,36 @@ def tile_gep_pb_t_kernel(tc, target_grad, embedding, bases0, bases1, bases2, out
         def flip(s):
             grouped = grouped_pool.tile([P, STEP_UNITS * K_GROUP], BF16, align_bytes=64)
             grouped_of[s] = grouped
-            for bank in range(STEP_BANKS):
-                flip_units(e_raw[s], grouped, bank * BANK_UNITS, BANK_UNITS)
+            for unit in range(0, STEP_UNITS, FLIP_UNITS):
+                flip_units(e_raw[s * STEP_LOADS + unit // LOAD_UNITS], unit % LOAD_UNITS, grouped, unit, FLIP_UNITS)
 
         def quantise(s):
             codes = mx_pool.tile([P, STEP_UNITS * P], U32, align_bytes=64)
             scales = mx_pool.tile([P, STEP_UNITS * P], U8, align_bytes=64)
             codes_of[s] = codes
             scales_of[s] = scales
-            for bank in range(STEP_BANKS):
-                quantise_units(grouped_of[s], codes, scales, bank * BANK_UNITS, BANK_UNITS)
+            for unit in range(0, STEP_UNITS, FLIP_UNITS):
+                quantise_units(grouped_of[s], codes, scales, unit, FLIP_UNITS)
 
         def multiply(s):
-            resid = resid_pool.tile([P, STEP_TILES * J_ALL], F32)
+            resid = resid_pool.tile([P, STEP_COLS], F32)
             resid_of[s] = resid
-            for t in range(STEP_TILES):
-                approx = approx_psum.tile([P, J_ALL], F32)
-                for g in range(GROUPS):
-                    unit_cols = slice((t * GROUPS + g) * P, (t * GROUPS + g + 1) * P)
-                    g_cols = slice(g * P, (g + 1) * P)
+            for first_unit in range(0, STEP_UNITS, PRODUCT_UNITS):
+                approx = approx_psum.tile([P, BANK_COLS], F32)
+                for n in range(PRODUCT_UNITS):
+                    unit_cols = slice((first_unit + n) * P, (first_unit + n + 1) * P)
+                    g = (first_unit + n) % GROUPS
                     nc.tensor.matmul_mx(
-                        out=approx[:, g_cols],
+                        out=approx[:, n * P : (n + 1) * P],
                         lhsT=codes_of[s][:, unit_cols].bitcast(FP8X4),
                         lhsT_scale=scales_of[s][:, unit_cols],
-                        rhs=b_codes[:, g_cols].bitcast(FP8X4),
-                        rhs_scale=b_scales[:, g_cols],
+                        rhs=b_codes[:, g * P : (g + 1) * P].bitcast(FP8X4),
+                        rhs_scale=b_scales[:, g * P : (g + 1) * P],
                         start=True,
                         stop=True,
                     )
-                t_cols = slice(t * J_ALL, (t + 1) * J_ALL)
-                nc.vector.tensor_tensor(out=resid[:, t_cols], in0=g_raw[s][:, t_cols], in1=approx[:], op=ALU.subtract)
+                cols = slice(first_unit * P, first_unit * P + BANK_COLS)
+                nc.vector.tensor_tensor(out=resid[:, cols], in0=g_raw[s][:, cols], in1=approx[:], op=ALU.subtract)
 
         def square(s):
             sumsq = small_pool.tile([P, STEP_TILES], F32)
@@ -165,10 +171,10 @@ def tile_gep_pb_t_kernel(tc, target_grad, embedding, bases0, bases1, bases2, out
         def weigh(s):
             for t in range(STEP_TILES):
                 nc.vector.scalar_tensor_tensor(
-                    out=weighted[t][:],
+                    out=weighted[t % 2][:],
                     in0=resid_of[s][:, t * J_ALL : (t + 1) * J_ALL],
                     scalar=factor_of[s][:, t : t + 1],
-                    in1=weighted[t][:],
+                    in1=weighted[t % 2][:],
                     op0=ALU.mult,
                     op1=ALU.add,
                 )
@@ -176,18 +182,17 @@ def tile_gep_pb_t_kernel(tc, target_grad, embedding, bases0, bases1, bases2, out
         for turn in range(STEPS + WEIGH_LAG):
             if 0 <= turn - QUANTISE_LAG < STEPS:
                 quantise(turn - QUANTISE_LAG)
-            if turn < STEPS:
-                flip(turn)
             if 0 <= turn - MULTIPLY_LAG < STEPS:
                 multiply(turn - MULTIPLY_LAG)
+            if turn < STEPS:
+                flip(turn)
             if 0 <= turn - SQUARE_LAG < STEPS:
                 square(turn - SQUARE_LAG)
                 clip_factor(turn - SQUARE_LAG)
             if 0 <= turn - WEIGH_LAG < STEPS:
                 weigh(turn - WEIGH_LAG)
 
-        for t in range(1, STEP_TILES):
-            nc.vector.tensor_tensor(out=weighted[0][:], in0=weighted[0][:], in1=weighted[t][:], op=ALU.add)
+        nc.vector.tensor_tensor(out=weighted[0][:], in0=weighted[0][:], in1=weighted[1][:], op=ALU.add)
         column_sums = approx_psum.tile([P, J_ALL], F32, tag="approx")
         nc.tensor.matmul(out=column_sums[:], lhsT=ones[:], rhs=weighted[0][:], start=True, stop=True)
         mean = const.tile([P, J_ALL], F32)

@@ -10,6 +10,7 @@ U8 = mybir.dt.uint8
 FP8X4 = mybir.dt.float8_e4m3fn_x4
 ALU = mybir.AluOpType
 ACT = mybir.ActivationFunctionType
+AXIS = mybir.AxisListType
 
 P = 128
 BATCH = 4096
@@ -18,21 +19,19 @@ K_GROUP = 512
 K_ALL = GROUPS * K_GROUP
 J_ALL = GROUPS * P
 TILES = BATCH // P
-STEP_TILES = 4
+STEP_TILES = 2
 STEPS = TILES // STEP_TILES
 STEP_UNITS = STEP_TILES * GROUPS
-STEP_COLS = STEP_TILES * J_ALL
 UNIT_WORDS = K_GROUP // 2
-FLIP_UNITS = 2
-LOAD_TILES = 2
-LOAD_UNITS = LOAD_TILES * GROUPS
-STEP_LOADS = STEP_TILES // LOAD_TILES
-BANK_COLS = 512
-PRODUCT_UNITS = BANK_COLS // P
+BANK_UNITS = 2
+STEP_BANKS = STEP_UNITS // BANK_UNITS
+GRAD_LOAD_STEPS = 4
 QUANTISE_LAG = 1
 MULTIPLY_LAG = 2
-SQUARE_LAG = 2
-WEIGH_LAG = 4
+SQUARE_LAG = 3
+SCALE_LAG = 4
+ADD_LAG = 5
+VECTOR_COPY_EVERY = 4
 
 FLOPS = 2 * BATCH * K_ALL * P
 
@@ -42,14 +41,15 @@ def tile_gep_pb_t_kernel(tc, target_grad, embedding, bases0, bases1, bases2, out
     with ExitStack() as ctx:
         ctx.enter_context(tc.manual_schedule())
         const = ctx.enter_context(tc.tile_pool(name="const", bufs=1))
-        e_pool = ctx.enter_context(tc.tile_pool(name="e_pool", bufs=STEPS * STEP_LOADS))
-        g_pool = ctx.enter_context(tc.tile_pool(name="g_pool", bufs=STEPS))
-        grouped_pool = ctx.enter_context(tc.tile_pool(name="grouped_pool", bufs=2))
+        e_pool = ctx.enter_context(tc.tile_pool(name="e_pool", bufs=STEPS))
+        g_pool = ctx.enter_context(tc.tile_pool(name="g_pool", bufs=STEPS // GRAD_LOAD_STEPS))
+        grouped_pool = ctx.enter_context(tc.tile_pool(name="grouped_pool", bufs=3))
         mx_pool = ctx.enter_context(tc.tile_pool(name="mx_pool", bufs=3))
-        resid_pool = ctx.enter_context(tc.tile_pool(name="resid_pool", bufs=WEIGH_LAG - MULTIPLY_LAG + 2))
+        resid_pool = ctx.enter_context(tc.tile_pool(name="resid_pool", bufs=ADD_LAG - MULTIPLY_LAG + 3))
         small_pool = ctx.enter_context(tc.tile_pool(name="small_pool", bufs=5))
-        flip_psum = ctx.enter_context(tc.psum_pool(name="flip_psum", bufs=5))
+        flip_psum = ctx.enter_context(tc.psum_pool(name="flip_psum", bufs=4))
         approx_psum = ctx.enter_context(tc.psum_pool(name="approx_psum", bufs=3))
+        sums_psum = ctx.enter_context(tc.psum_pool(name="sums_psum", bufs=1))
 
         emb_rows = embedding.rearrange("(p t) k -> p (t k)", t=TILES)
         grad_rows = target_grad.rearrange("(p t) j -> p (t j)", t=TILES)
@@ -59,38 +59,38 @@ def tile_gep_pb_t_kernel(tc, target_grad, embedding, bases0, bases1, bases2, out
         e_raw = []
         g_raw = []
         for s in range(STEPS):
-            for load in range(s * STEP_LOADS, (s + 1) * STEP_LOADS):
-                e_load = e_pool.tile([P, LOAD_TILES * K_ALL], BF16)
-                nc.sync.dma_start(out=e_load[:], in_=emb_rows[:, load * LOAD_TILES * K_ALL : (load + 1) * LOAD_TILES * K_ALL])
-                e_raw.append(e_load)
-            g_step = g_pool.tile([P, STEP_COLS], BF16)
-            nc.sync.dma_start(out=g_step[:], in_=grad_rows[:, s * STEP_COLS : (s + 1) * STEP_COLS])
-            g_raw.append(g_step)
+            e_step = e_pool.tile([P, STEP_TILES * K_ALL], BF16)
+            nc.sync.dma_start(out=e_step[:], in_=emb_rows[:, s * STEP_TILES * K_ALL : (s + 1) * STEP_TILES * K_ALL])
+            e_raw.append(e_step)
+            if s % GRAD_LOAD_STEPS == 1:
+                g_cols = GRAD_LOAD_STEPS * STEP_TILES * J_ALL
+                g_load = g_pool.tile([P, g_cols], BF16)
+                nc.sync.dma_start(out=g_load[:], in_=grad_rows[:, len(g_raw) * g_cols : (len(g_raw) + 1) * g_cols])
+                g_raw.append(g_load)
 
         ident = const.tile([P, P], F32)
         make_identity(nc, ident[:])
-        ones = const.tile([P, P], F32)
-        nc.vector.memset(ones[:], 1.0)
-        weighted = []
-        for t in range(2):
-            weighted_t = const.tile([P, J_ALL], F32, name="weighted_%d" % t)
-            nc.vector.memset(weighted_t[:], 0.0)
-            weighted.append(weighted_t)
-        minus_half = const.tile([P, STEP_TILES], F32)
-        nc.gpsimd.memset(minus_half[:], -0.5)
+        totals = const.tile([P, P], F32)
+        nc.vector.memset(totals[:], 0.0)
+        warm = const.tile([P, 1], F32)
+        nc.vector.memset(warm[:], 1.0)
+        nc.scalar.activation(out=warm[:], in_=warm[:], func=ACT.Abs_reciprocal_sqrt)
 
-        def flip_units(src, src_unit, grouped, first_unit, n_units):
+        def flip_units(src, grouped, first_unit, n_units, on_vector):
             src_words = src[:].bitcast(F32)
             grouped_words = grouped[:].bitcast(F32)
-            flipped = flip_psum.tile([P, FLIP_UNITS, 2, P], F32)
+            flipped = flip_psum.tile([P, BANK_UNITS, 2, P], F32)
             for n in range(n_units):
                 for h in range(2):
-                    first_word = (src_unit + n) * UNIT_WORDS + h * P
+                    first_word = (first_unit + n) * UNIT_WORDS + h * P
                     nc.tensor.transpose(flipped[:, n, h, :], src_words[:, first_word : first_word + P], ident[:])
             dst = grouped_words[:, first_unit * UNIT_WORDS : (first_unit + n_units) * UNIT_WORDS]
             dst = dst.rearrange("p (n r h) -> p n r h", n=n_units, h=2)
             flipped_rows = flipped[:, 0:n_units, :, :].rearrange("p n h r -> p n r h")
-            nc.scalar.copy(out=dst, in_=flipped_rows)
+            if on_vector:
+                nc.vector.tensor_copy(out=dst, in_=flipped_rows)
+            else:
+                nc.scalar.copy(out=dst, in_=flipped_rows)
 
         def quantise_units(grouped, codes, scales, first_unit, n_units):
             cols = slice(first_unit * P, (first_unit + n_units) * P)
@@ -104,7 +104,7 @@ def tile_gep_pb_t_kernel(tc, target_grad, embedding, bases0, bases1, bases2, out
         b_codes = const.tile([P, J_ALL], U32, align_bytes=64)
         b_scales = const.tile([P, J_ALL], U8, align_bytes=64)
         for g in range(GROUPS):
-            flip_units(b_raw, g, b_grouped, g, 1)
+            flip_units(b_raw, b_grouped, g, 1, False)
         for g in range(GROUPS):
             quantise_units(b_grouped, b_codes, b_scales, g, 1)
 
@@ -114,40 +114,47 @@ def tile_gep_pb_t_kernel(tc, target_grad, embedding, bases0, bases1, bases2, out
         resid_of = {}
         sumsq_of = {}
         factor_of = {}
+        flipped_sums = sums_psum.tile([P, GROUPS, P], F32)
 
         def flip(s):
             grouped = grouped_pool.tile([P, STEP_UNITS * K_GROUP], BF16, align_bytes=64)
             grouped_of[s] = grouped
-            for unit in range(0, STEP_UNITS, FLIP_UNITS):
-                flip_units(e_raw[s * STEP_LOADS + unit // LOAD_UNITS], unit % LOAD_UNITS, grouped, unit, FLIP_UNITS)
+            for bank in range(STEP_BANKS):
+                on_vector = (s * STEP_BANKS + bank) % VECTOR_COPY_EVERY == VECTOR_COPY_EVERY - 1
+                flip_units(e_raw[s], grouped, bank * BANK_UNITS, BANK_UNITS, on_vector)
 
         def quantise(s):
             codes = mx_pool.tile([P, STEP_UNITS * P], U32, align_bytes=64)
             scales = mx_pool.tile([P, STEP_UNITS * P], U8, align_bytes=64)
             codes_of[s] = codes
             scales_of[s] = scales
-            for unit in range(0, STEP_UNITS, FLIP_UNITS):
-                quantise_units(grouped_of[s], codes, scales, unit, FLIP_UNITS)
+            for bank in range(STEP_BANKS):
+                quantise_units(grouped_of[s], codes, scales, bank * BANK_UNITS, BANK_UNITS)
 
         def multiply(s):
-            resid = resid_pool.tile([P, STEP_COLS], F32)
+            resid = resid_pool.tile([P, STEP_TILES * J_ALL], F32)
             resid_of[s] = resid
-            for first_unit in range(0, STEP_UNITS, PRODUCT_UNITS):
-                approx = approx_psum.tile([P, BANK_COLS], F32)
-                for n in range(PRODUCT_UNITS):
-                    unit_cols = slice((first_unit + n) * P, (first_unit + n + 1) * P)
-                    g = (first_unit + n) % GROUPS
+            for t in range(STEP_TILES):
+                approx = approx_psum.tile([P, J_ALL], F32)
+                for g in range(GROUPS):
+                    unit_cols = slice((t * GROUPS + g) * P, (t * GROUPS + g + 1) * P)
+                    g_cols = slice(g * P, (g + 1) * P)
                     nc.tensor.matmul_mx(
-                        out=approx[:, n * P : (n + 1) * P],
+                        out=approx[:, g_cols],
                         lhsT=codes_of[s][:, unit_cols].bitcast(FP8X4),
                         lhsT_scale=scales_of[s][:, unit_cols],
-                        rhs=b_codes[:, g * P : (g + 1) * P].bitcast(FP8X4),
-                        rhs_scale=b_scales[:, g * P : (g + 1) * P],
+                        rhs=b_codes[:, g_cols].bitcast(FP8X4),
+                        rhs_scale=b_scales[:, g_cols],
                         start=True,
                         stop=True,
                     )
-                cols = slice(first_unit * P, first_unit * P + BANK_COLS)
-                nc.vector.tensor_tensor(out=resid[:, cols], in0=g_raw[s][:, cols], in1=approx[:], op=ALU.subtract)
+                grad_first = ((s % GRAD_LOAD_STEPS) * STEP_TILES + t) * J_ALL
+                nc.vector.tensor_tensor(
+                    out=resid[:, t * J_ALL : (t + 1) * J_ALL],
+                    in0=g_raw[s // GRAD_LOAD_STEPS][:, grad_first : grad_first + J_ALL],
+                    in1=approx[:],
+                    op=ALU.subtract,
+                )
 
         def square(s):
             sumsq = small_pool.tile([P, STEP_TILES], F32)
@@ -162,39 +169,50 @@ def tile_gep_pb_t_kernel(tc, target_grad, embedding, bases0, bases1, bases2, out
                 )
 
         def clip_factor(s):
-            floored = small_pool.tile([P, STEP_TILES], F32)
-            nc.gpsimd.tensor_scalar_max(out=floored[:], in0=sumsq_of[s][:], scalar1=1.0)
+            excess = small_pool.tile([P, STEP_TILES], F32)
+            nc.scalar.activation(out=excess[:], in_=sumsq_of[s][:], func=ACT.Relu, bias=-1.0)
             factor = small_pool.tile([P, STEP_TILES], F32)
-            nc.gpsimd.tensor_tensor(out=factor[:], in0=floored[:], in1=minus_half[:], op=ALU.pow)
+            nc.scalar.activation(out=factor[:], in_=excess[:], func=ACT.Abs_reciprocal_sqrt, bias=1.0)
             factor_of[s] = factor
 
-        def weigh(s):
+        def scale(s):
             for t in range(STEP_TILES):
-                nc.vector.scalar_tensor_tensor(
-                    out=weighted[t % 2][:],
-                    in0=resid_of[s][:, t * J_ALL : (t + 1) * J_ALL],
-                    scalar=factor_of[s][:, t : t + 1],
-                    in1=weighted[t % 2][:],
-                    op0=ALU.mult,
-                    op1=ALU.add,
+                resid_t = resid_of[s][:, t * J_ALL : (t + 1) * J_ALL]
+                nc.gpsimd.tensor_scalar(
+                    out=resid_t, in0=resid_t, scalar1=factor_of[s][:, t : t + 1], scalar2=0.0, op0=ALU.mult, op1=ALU.add
                 )
 
-        for turn in range(STEPS + WEIGH_LAG):
+        def add_up(s):
+            for t in range(STEP_TILES):
+                for g in range(GROUPS):
+                    unit_cols = slice((t * GROUPS + g) * P, (t * GROUPS + g + 1) * P)
+                    nc.tensor.matmul(
+                        out=flipped_sums[:, g, :],
+                        lhsT=resid_of[s][:, unit_cols],
+                        rhs=ident[:],
+                        is_transpose=True,
+                        start=(s == 0 and t == 0 and g == 0),
+                        stop=(s == STEPS - 1 and t == STEP_TILES - 1 and g == GROUPS - 1),
+                    )
+
+        for turn in range(STEPS + ADD_LAG):
             if 0 <= turn - QUANTISE_LAG < STEPS:
                 quantise(turn - QUANTISE_LAG)
-            if 0 <= turn - MULTIPLY_LAG < STEPS:
-                multiply(turn - MULTIPLY_LAG)
             if turn < STEPS:
                 flip(turn)
+            if 0 <= turn - MULTIPLY_LAG < STEPS:
+                multiply(turn - MULTIPLY_LAG)
             if 0 <= turn - SQUARE_LAG < STEPS:
                 square(turn - SQUARE_LAG)
                 clip_factor(turn - SQUARE_LAG)
-            if 0 <= turn - WEIGH_LAG < STEPS:
-                weigh(turn - WEIGH_LAG)
+            if 0 <= turn - SCALE_LAG < STEPS:
+                scale(turn - SCALE_LAG)
+            if 0 <= turn - ADD_LAG < STEPS:
+                add_up(turn - ADD_LAG)
 
-        nc.vector.tensor_tensor(out=weighted[0][:], in0=weighted[0][:], in1=weighted[1][:], op=ALU.add)
-        column_sums = approx_psum.tile([P, J_ALL], F32, tag="approx")
-        nc.tensor.matmul(out=column_sums[:], lhsT=ones[:], rhs=weighted[0][:], start=True, stop=True)
-        mean = const.tile([P, J_ALL], F32)
-        nc.scalar.mul(out=mean[:], in_=column_sums[:], mul=1.0 / BATCH)
-        nc.sync.dma_start(out=out.rearrange("(o j) -> o j", o=1), in_=mean[0:1, :])
+        nc.vector.tensor_reduce(out=totals[:, 0:GROUPS], in_=flipped_sums[:], axis=AXIS.X, op=ALU.add)
+        totals_flipped = flip_psum.tile([P, P], F32, tag="flipped")
+        nc.tensor.transpose(totals_flipped[:], totals[:], ident[:])
+        mean = const.tile([P, P], F32)
+        nc.scalar.mul(out=mean[:], in_=totals_flipped[:], mul=1.0 / BATCH)
+        nc.sync.dma_start(out=out.rearrange("(g j) -> g j", g=GROUPS), in_=mean[0:GROUPS, :])

from contextlib import ExitStack

import concourse.mybir as mybir
from concourse.masks import make_identity

F32 = mybir.dt.float32
BF16 = mybir.dt.bfloat16
U32 = mybir.dt.uint32
U8 = mybir.dt.uint8
FP8X4 = mybir.dt.float8_e4m3fn_x4
ALU = mybir.AluOpType
ACT = mybir.ActivationFunctionType
AXIS = mybir.AxisListType

P = 128
BATCH = 4096
GROUPS = 3
K_GROUP = 512
K_ALL = GROUPS * K_GROUP
J_ALL = GROUPS * P
TILES = BATCH // P
STEP_TILES = 2
STEPS = TILES // STEP_TILES
STEP_UNITS = STEP_TILES * GROUPS
UNIT_WORDS = K_GROUP // 2
BANK_UNITS = 2
STEP_BANKS = STEP_UNITS // BANK_UNITS
GRAD_LOAD_STEPS = 4
QUANTISE_LAG = 1
MULTIPLY_LAG = 2
SQUARE_LAG = 3
SCALE_LAG = 4
ADD_LAG = 5
VECTOR_COPY_EVERY = 4

FLOPS = 2 * BATCH * K_ALL * P


def tile_gep_pb_t_kernel(tc, target_grad, embedding, bases0, bases1, bases2, out):
    nc = tc.nc
    with ExitStack() as ctx:
        ctx.enter_context(tc.manual_schedule())
        const = ctx.enter_context(tc.tile_pool(name="const", bufs=1))
        e_pool = ctx.enter_context(tc.tile_pool(name="e_pool", bufs=STEPS))
        g_pool = ctx.enter_context(tc.tile_pool(name="g_pool", bufs=STEPS // GRAD_LOAD_STEPS))
        grouped_pool = ctx.enter_context(tc.tile_pool(name="grouped_pool", bufs=3))
        mx_pool = ctx.enter_context(tc.tile_pool(name="mx_pool", bufs=3))
        resid_pool = ctx.enter_context(tc.tile_pool(name="resid_pool", bufs=ADD_LAG - MULTIPLY_LAG + 3))
        small_pool = ctx.enter_context(tc.tile_pool(name="small_pool", bufs=5))
        flip_psum = ctx.enter_context(tc.psum_pool(name="flip_psum", bufs=4))
        approx_psum = ctx.enter_context(tc.psum_pool(name="approx_psum", bufs=3))
        sums_psum = ctx.enter_context(tc.psum_pool(name="sums_psum", bufs=1))

        emb_rows = embedding.rearrange("(p t) k -> p (t k)", t=TILES)
        grad_rows = target_grad.rearrange("(p t) j -> p (t j)", t=TILES)
        b_raw = const.tile([P, K_ALL], BF16)
        for g, bases in enumerate((bases0, bases1, bases2)):
            nc.scalar.dma_start(out=b_raw[:, g * K_GROUP : (g + 1) * K_GROUP], in_=bases)
        e_raw = []
        g_raw = []
        for s in range(STEPS):
            e_step = e_pool.tile([P, STEP_TILES * K_ALL], BF16)
            nc.sync.dma_start(out=e_step[:], in_=emb_rows[:, s * STEP_TILES * K_ALL : (s + 1) * STEP_TILES * K_ALL])
            e_raw.append(e_step)
            if s % GRAD_LOAD_STEPS == 1:
                g_cols = GRAD_LOAD_STEPS * STEP_TILES * J_ALL
                g_load = g_pool.tile([P, g_cols], BF16)
                nc.sync.dma_start(out=g_load[:], in_=grad_rows[:, len(g_raw) * g_cols : (len(g_raw) + 1) * g_cols])
                g_raw.append(g_load)

        ident = const.tile([P, P], F32)
        make_identity(nc, ident[:])
        totals = const.tile([P, P], F32)
        nc.vector.memset(totals[:], 0.0)
        warm = const.tile([P, 1], F32)
        nc.vector.memset(warm[:], 1.0)
        nc.scalar.activation(out=warm[:], in_=warm[:], func=ACT.Abs_reciprocal_sqrt)

        def flip_units(src, grouped, first_unit, n_units, on_vector):
            src_words = src[:].bitcast(F32)
            grouped_words = grouped[:].bitcast(F32)
            flipped = flip_psum.tile([P, BANK_UNITS, 2, P], F32)
            for n in range(n_units):
                for h in range(2):
                    first_word = (first_unit + n) * UNIT_WORDS + h * P
                    nc.tensor.transpose(flipped[:, n, h, :], src_words[:, first_word : first_word + P], ident[:])
            dst = grouped_words[:, first_unit * UNIT_WORDS : (first_unit + n_units) * UNIT_WORDS]
            dst = dst.rearrange("p (n r h) -> p n r h", n=n_units, h=2)
            flipped_rows = flipped[:, 0:n_units, :, :].rearrange("p n h r -> p n r h")
            if on_vector:
                nc.vector.tensor_copy(out=dst, in_=flipped_rows)
            else:
                nc.scalar.copy(out=dst, in_=flipped_rows)

        def quantise_units(grouped, codes, scales, first_unit, n_units):
            cols = slice(first_unit * P, (first_unit + n_units) * P)
            nc.vector.quantize_mx(
                out=codes[:, cols].bitcast(FP8X4),
                scales=scales[:, cols],
                in_=grouped[:, first_unit * K_GROUP : (first_unit + n_units) * K_GROUP],
            )

        b_grouped = const.tile([P, K_ALL], BF16, align_bytes=64)
        b_codes = const.tile([P, J_ALL], U32, align_bytes=64)
        b_scales = const.tile([P, J_ALL], U8, align_bytes=64)
        for g in range(GROUPS):
            flip_units(b_raw, b_grouped, g, 1, False)
        for g in range(GROUPS):
            quantise_units(b_grouped, b_codes, b_scales, g, 1)

        grouped_of = {}
        codes_of = {}
        scales_of = {}
        resid_of = {}
        sumsq_of = {}
        factor_of = {}
        flipped_sums = sums_psum.tile([P, GROUPS, P], F32)

        def flip(s):
            grouped = grouped_pool.tile([P, STEP_UNITS * K_GROUP], BF16, align_bytes=64)
            grouped_of[s] = grouped
            for bank in range(STEP_BANKS):
                on_vector = (s * STEP_BANKS + bank) % VECTOR_COPY_EVERY == VECTOR_COPY_EVERY - 1
                flip_units(e_raw[s], grouped, bank * BANK_UNITS, BANK_UNITS, on_vector)

        def quantise(s):
            codes = mx_pool.tile([P, STEP_UNITS * P], U32, align_bytes=64)
            scales = mx_pool.tile([P, STEP_UNITS * P], U8, align_bytes=64)
            codes_of[s] = codes
            scales_of[s] = scales
            for bank in range(STEP_BANKS):
                quantise_units(grouped_of[s], codes, scales, bank * BANK_UNITS, BANK_UNITS)

        def multiply(s):
            resid = resid_pool.tile([P, STEP_TILES * J_ALL], F32)
            resid_of[s] = resid
            for t in range(STEP_TILES):
                approx = approx_psum.tile([P, J_ALL], F32)
                for g in range(GROUPS):
                    unit_cols = slice((t * GROUPS + g) * P, (t * GROUPS + g + 1) * P)
                    g_cols = slice(g * P, (g + 1) * P)
                    nc.tensor.matmul_mx(
                        out=approx[:, g_cols],
                        lhsT=codes_of[s][:, unit_cols].bitcast(FP8X4),
                        lhsT_scale=scales_of[s][:, unit_cols],
                        rhs=b_codes[:, g_cols].bitcast(FP8X4),
                        rhs_scale=b_scales[:, g_cols],
                        start=True,
                        stop=True,
                    )
                grad_first = ((s % GRAD_LOAD_STEPS) * STEP_TILES + t) * J_ALL
                nc.vector.tensor_tensor(
                    out=resid[:, t * J_ALL : (t + 1) * J_ALL],
                    in0=g_raw[s // GRAD_LOAD_STEPS][:, grad_first : grad_first + J_ALL],
                    in1=approx[:],
                    op=ALU.subtract,
                )

        def square(s):
            sumsq = small_pool.tile([P, STEP_TILES], F32)
            sumsq_of[s] = sumsq
            for t in range(STEP_TILES):
                squares = small_pool.tile([P, J_ALL], BF16)
                nc.scalar.activation(
                    out=squares[:],
                    in_=resid_of[s][:, t * J_ALL : (t + 1) * J_ALL],
                    func=ACT.Square,
                    accum_out=sumsq[:, t : t + 1],
                )

        def clip_factor(s):
            excess = small_pool.tile([P, STEP_TILES], F32)
            nc.scalar.activation(out=excess[:], in_=sumsq_of[s][:], func=ACT.Relu, bias=-1.0)
            factor = small_pool.tile([P, STEP_TILES], F32)
            nc.scalar.activation(out=factor[:], in_=excess[:], func=ACT.Abs_reciprocal_sqrt, bias=1.0)
            factor_of[s] = factor

        def scale(s):
            for t in range(STEP_TILES):
                resid_t = resid_of[s][:, t * J_ALL : (t + 1) * J_ALL]
                nc.gpsimd.tensor_scalar(
                    out=resid_t, in0=resid_t, scalar1=factor_of[s][:, t : t + 1], scalar2=0.0, op0=ALU.mult, op1=ALU.add
                )

        def add_up(s):
            for t in range(STEP_TILES):
                for g in range(GROUPS):
                    unit_cols = slice((t * GROUPS + g) * P, (t * GROUPS + g + 1) * P)
                    nc.tensor.matmul(
                        out=flipped_sums[:, g, :],
                        lhsT=resid_of[s][:, unit_cols],
                        rhs=ident[:],
                        is_transpose=True,
                        start=(s == 0 and t == 0 and g == 0),
                        stop=(s == STEPS - 1 and t == STEP_TILES - 1 and g == GROUPS - 1),
                    )

        for turn in range(STEPS + ADD_LAG):
            if 0 <= turn - QUANTISE_LAG < STEPS:
                quantise(turn - QUANTISE_LAG)
            if turn < STEPS:
                flip(turn)
            if 0 <= turn - MULTIPLY_LAG < STEPS:
                multiply(turn - MULTIPLY_LAG)
            if 0 <= turn - SQUARE_LAG < STEPS:
                square(turn - SQUARE_LAG)
                clip_factor(turn - SQUARE_LAG)
            if 0 <= turn - SCALE_LAG < STEPS:
                scale(turn - SCALE_LAG)
            if 0 <= turn - ADD_LAG < STEPS:
                add_up(turn - ADD_LAG)

        nc.vector.tensor_reduce(out=totals[:, 0:GROUPS], in_=flipped_sums[:], axis=AXIS.X, op=ALU.add)
        totals_flipped = flip_psum.tile([P, P], F32, tag="flipped")
        nc.tensor.transpose(totals_flipped[:], totals[:], ident[:])
        mean = const.tile([P, P], F32)
        nc.scalar.mul(out=mean[:], in_=totals_flipped[:], mul=1.0 / BATCH)
        nc.sync.dma_start(out=out.rearrange("(g j) -> g j", g=GROUPS), in_=mean[0:GROUPS, :])
